import numpy as np
import ml_dtypes


def mxq(x, axis, fmt="e4m3"):
    dtype, down = {"e4m3": (ml_dtypes.float8_e4m3fn, 7), "e5m2": (ml_dtypes.float8_e5m2, 14)}[fmt]
    v = np.moveaxis(np.asarray(x, np.float32).astype(ml_dtypes.bfloat16).astype(np.float64), axis, -1)
    blocks = v.reshape(v.shape[:-1] + (-1, 32))
    amax = np.abs(blocks).max(-1, keepdims=True)
    byte = np.maximum(np.where(amax > 0, np.frexp(amax)[1] - 1 + 127, 0) - down, 1)
    scale = np.exp2(byte - 127.0)
    codes = (blocks / scale).astype(np.float32).astype(dtype).astype(np.float64)
    return np.moveaxis((codes * scale).reshape(v.shape), -1, axis)


WIDE = False


def mx_kscale(k):
    if not WIDE:
        return np.ones(k)
    levels = np.array([10, -10, 5, -5, 0])
    if k % 512:
        return np.exp2(np.random.permutation(np.resize(levels, k // 32))).repeat(32)
    a = np.empty((k // 512, 16))
    for p in range(k // 512):
        a[p, :8] = np.random.permutation(np.resize(levels, 8))
        for g in range(8):
            far = levels[np.abs(levels - a[p, g]) >= 10]
            a[p, g + 8] = far[np.random.randint(len(far))]
    return np.exp2(a.ravel()).repeat(32)


BF16 = ml_dtypes.bfloat16


def bf(x):
    return np.asarray(x, np.float32).astype(BF16)


def f64(x):
    return np.asarray(x).astype(np.float64)


B, C, H, W = 8, 512, 16, 32
N = H * W
SIG = 3.0


def draw0():
    s, t = mx_kscale(C), mx_kscale(C)
    r = np.sqrt(SIG / np.sqrt(C))
    return {
        "q_ir": bf(np.random.standard_normal((B, C, N)) * r / t[:, None]),
        "irSegF": bf(np.random.standard_normal((B, C, H, W)) * s[:, None, None]),
        "Wk_dr": bf(np.random.standard_normal((C, C)) * r / np.sqrt(C) * t[:, None] / s[None, :]),
        "bk_dr": bf(np.random.standard_normal(C) * 0.1 * t),
    }


def core(q_ir, irSegF, Wk_dr, bk_dr):
    seg = f64(irSegF).reshape(B, C, N)
    key = (mxq(f64(Wk_dr), 1, "e4m3") @ mxq(seg, 1, "e4m3")) + f64(bk_dr)[None, :, None]
    s = mxq(f64(q_ir), 1, "e4m3").transpose(0, 2, 1) @ mxq(key, 1, "e4m3")
    e = np.exp(s - s.max(1, keepdims=True))
    return e / e.sum(1, keepdims=True)


def e4m3fn_bytes(y):
    return np.clip(np.asarray(y, np.float64), -448.0, 448.0).astype(np.float32).astype(ml_dtypes.float8_e4m3fn).view(np.uint8)


def e4m3fn_values(b):
    return np.asarray(b, np.uint8).view(ml_dtypes.float8_e4m3fn).astype(np.float64)


def setup_inputs():
    d = draw0()
    x0 = np.asarray(d['q_ir']).astype(np.float64)
    s = (np.max(np.abs(x0), axis=(0, 2), keepdims=True) / 448.0).astype(np.float32)
    out = {}
    for k, v in d.items():
        if k == 'q_ir':
            out['q_ir_bytes'] = e4m3fn_bytes(x0 / s.astype(np.float64))
            out['q_ir_scale'] = s
        else:
            out[k] = v
    return out


def reference(q_ir_bytes, q_ir_scale, irSegF, Wk_dr, bk_dr):
    return core(e4m3fn_values(q_ir_bytes) * q_ir_scale.astype(np.float64), irSegF, Wk_dr, bk_dr)

@@ -1,0 +1,229 @@
+from contextlib import ExitStack
+
+import concourse.mybir as mybir
+from concourse.masks import make_identity
+
+B, C, N = 8, 512, 512
+FLOPS = 2 * 2 * B * C * C * N
+
+P = 128
+T = 4
+F32 = mybir.dt.float32
+BF16 = mybir.dt.bfloat16
+U32 = mybir.dt.uint32
+U8 = mybir.dt.uint8
+F8 = mybir.dt.float8_e4m3fn
+X4 = mybir.dt.float8_e4m3fn_x4
+ADD = mybir.AluOpType.add
+MULT = mybir.AluOpType.mult
+MAX = mybir.AluOpType.max
+ACT = mybir.ActivationFunctionType
+AX = mybir.AxisListType
+
+SLOTS = 4 * B
+FIRST = -12
+
+
+def tile_featuremaptransformer_pb_t_kernel(tc, q_ir_bytes, q_ir_scale, irSegF, Wk_dr, bk_dr, out):
+    nc = tc.nc
+    with ExitStack() as ctx:
+        keep = ctx.enter_context(tc.tile_pool(name="keep", bufs=1))
+        raw = ctx.enter_context(tc.tile_pool(name="raw", bufs=B))
+        prep = ctx.enter_context(tc.tile_pool(name="prep", bufs=3))
+        soft = ctx.enter_context(tc.tile_pool(name="soft", bufs=4))
+        ps_s = ctx.enter_context(tc.psum_pool(name="ps_s", bufs=3))
+        ps_k = ctx.enter_context(tc.psum_pool(name="ps_k", bufs=2))
+        ps_t = ctx.enter_context(tc.psum_pool(name="ps_t", bufs=3))
+        ctx.enter_context(tc.manual_schedule())
+
+        ident = keep.tile([P, P], F32, name="ident")
+        make_identity(nc, ident[:])
+
+        w_raw = keep.tile([P, T, C], BF16, name="w_raw")
+        w_rows = Wk_dr.rearrange("(m t) k -> m t k", t=T)
+        for h in range(2):
+            nc.sync.dma_start(out=w_raw[:, 2 * h : 2 * h + 2, :], in_=w_rows[:, 2 * h : 2 * h + 2, :])
+        q_scale = keep.tile([P, T], F32, name="q_scale")
+        bias = keep.tile([P, T], BF16, name="bias")
+        seg_raw, q_raw = [], []
+        for b in range(B):
+            seg_b = raw.tile([P, T, N], BF16, name="seg_b")
+            nc.sync.dma_start(out=seg_b[:], in_=irSegF[b].rearrange("(p t) h w -> p t (h w)", t=T))
+            seg_raw.append(seg_b)
+            if b == 0:
+                nc.sync.dma_start(out=q_scale[:], in_=q_ir_scale.rearrange("o (p t) x -> p (o t x)", t=T))
+                nc.sync.dma_start(out=bias[:], in_=bk_dr.rearrange("(p t) -> p t", t=T))
+            q_b = raw.tile([P, T, N], U8, name="q_b")
+            nc.sync.dma_start(out=q_b[:], in_=q_ir_bytes[b].rearrange("(p t) n -> p t n", t=T))
+            q_raw.append(q_b)
+
+        def quantize(grouped, codes, scales, lo, hi):
+            nc.vector.quantize_mx(
+                out=codes[:, lo:hi].bitcast(X4),
+                scales=scales[:, lo:hi],
+                in_=grouped[:].rearrange("p c t -> p (c t)")[:, T * lo : T * hi],
+            )
+
+        def interleave(vector, grouped, planes, u):
+            cols = slice(P * u, P * (u + 1))
+            dst = grouped[:, cols, :].rearrange("p (c i) t -> p c t i", i=4)
+            src = planes[:, :, cols].rearrange("p t (c i) -> p c t i", i=4)
+            if vector:
+                nc.vector.tensor_copy(out=dst, in_=src)
+            else:
+                nc.scalar.copy(out=dst, in_=src)
+
+        w_grouped = keep.tile([P, C, T], BF16, align_bytes=64, name="w_grouped")
+        w_codes = keep.tile([P, C], U32, align_bytes=64, name="w_codes")
+        w_scales = keep.tile([P, C], U8, align_bytes=64, name="w_scales")
+        w_words = w_grouped[:].rearrange("p o j -> p (o j)").bitcast(F32)
+        for h in range(2):
+            turned = ps_t.tile([P, 4, P], F32, name="turned")
+            for j in range(4):
+                t, u = 2 * h + j // 2, j % 2
+                words = w_raw[:, t, :].bitcast(F32)
+                nc.tensor.transpose(turned[:, j, :], words[:, u : C // 2 : 2], ident[:])
+            dst = w_words[:, 512 * h : 512 * (h + 1)].rearrange("p (t m u) -> p t m u", t=2, u=2)
+            src = turned[:].rearrange("p (t u) m -> p t m u", u=2)
+            if h == 0:
+                nc.scalar.copy(out=dst, in_=src)
+            else:
+                nc.vector.tensor_copy(out=dst, in_=src)
+
+        seg_grouped, seg_codes, seg_scales = {}, {}, {}
+        q_wide, q_grouped, q_codes, q_scales = {}, {}, {}, {}
+        key_psum, key_grouped, key_codes, key_scales = {}, {}, {}, {}
+        score, exps, negmax, total, recip, turned_e, result = {}, {}, {}, {}, {}, {}, {}
+
+        def seg_unit(x):
+            b, u = divmod(x, 4)
+            if u == 0:
+                seg_grouped[b] = prep.tile([P, N, T], BF16, align_bytes=64, name="seg_grouped_b")
+                seg_codes[b] = prep.tile([P, N], U32, align_bytes=64, name="seg_codes_b")
+                seg_scales[b] = prep.tile([P, N], U8, align_bytes=64, name="seg_scales_b")
+            interleave(b == 0 and u % 2 == 1, seg_grouped[b], seg_raw[b], u)
+
+        def widen_unit(x):
+            b, t = divmod(x, 4)
+            if t == 0:
+                q_wide[b] = prep.tile([P, T, N], BF16, align_bytes=64, name="q_wide_b")
+            nc.vector.tensor_scalar(
+                out=q_wide[b][:, t, :], in0=q_raw[b][:, t, :].bitcast(F8), scalar1=q_scale[:, t : t + 1], scalar2=None, op0=MULT
+            )
+
+        def q_unit(x):
+            b, u = divmod(x, 4)
+            if u == 0:
+                q_grouped[b] = prep.tile([P, N, T], BF16, align_bytes=64, name="q_grouped_b")
+                q_codes[b] = prep.tile([P, N], U32, align_bytes=64, name="q_codes_b")
+                q_scales[b] = prep.tile([P, N], U8, align_bytes=64, name="q_scales_b")
+            interleave(u == 3, q_grouped[b], q_wide[b], u)
+
+        def key_matmuls(x):
+            b, u = divmod(x, 4)
+            key_psum[x] = ps_k.tile([P, T, P], F32, name="key_psum_x")
+            cols = slice(P * u, P * (u + 1))
+            for t in range(T):
+                nc.tensor.matmul_mx(
+                    out=key_psum[x][:, t, :],
+                    lhsT=w_codes[:, P * t : P * (t + 1)].bitcast(X4),
+                    lhsT_scale=w_scales[:, P * t : P * (t + 1)],
+                    rhs=seg_codes[b][:, cols].bitcast(X4),
+                    rhs_scale=seg_scales[b][:, cols],
+                    start=True,
+                    stop=True,
+                )
+
+        def key_unit(x):
+            b, u = divmod(x, 4)
+            if u == 0:
+                key_grouped[b] = prep.tile([P, N, T], BF16, align_bytes=64, name="key_grouped_b")
+                key_codes[b] = prep.tile([P, N], U32, align_bytes=64, name="key_codes_b")
+                key_scales[b] = prep.tile([P, N], U8, align_bytes=64, name="key_scales_b")
+            nc.vector.tensor_tensor(
+                out=key_grouped[b][:, P * u : P * (u + 1), :],
+                in0=key_psum[x][:].rearrange("p t m -> p m t"),
+                in1=bias[:].unsqueeze(1).to_broadcast([P, P, T]),
+                op=ADD,
+            )
+
+        def score_matmul(x):
+            b, u = divmod(x, 4)
+            score[x] = ps_s.tile([P, N], F32, name="score_x")
+            cols = slice(P * u, P * (u + 1))
+            nc.tensor.matmul_mx(
+                out=score[x][:],
+                lhsT=key_codes[b][:, cols].bitcast(X4),
+                lhsT_scale=key_scales[b][:, cols],
+                rhs=q_codes[b][:].bitcast(X4),
+                rhs_scale=q_scales[b][:],
+                start=True,
+                stop=True,
+            )
+
+        def max_unit(x):
+            negmax[x] = soft.tile([P, 1], F32, name="negmax_x")
+            nc.vector.tensor_reduce(out=negmax[x][:], in_=score[x][:], axis=AX.X, op=MAX, negate=True)
+
+        def exp_unit(x):
+            exps[x] = soft.tile([P, N], F32, name="exps_x")
+            total[x] = soft.tile([P, 1], F32, name="total_x")
+            nc.scalar.activation(
+                out=exps[x][:], in_=score[x][:], func=ACT.Exp, bias=negmax[x][:], scale=1.0, accum_out=total[x][:]
+            )
+
+        def recip_unit(x):
+            recip[x] = soft.tile([P, 1], F32, name="recip_x")
+            nc.vector.reciprocal(out=recip[x][:], in_=total[x][:])
+
+        def norm_unit(x):
+            nc.vector.tensor_scalar(out=exps[x][:], in0=exps[x][:], scalar1=recip[x][:], scalar2=None, op0=MULT)
+
+        def turn_unit(x):
+            turned_e[x] = ps_t.tile([P, 4, P], F32, name="turned")
+            e = exps[x]
+            for j in range(4):
+                nc.tensor.transpose(turned_e[x][:, j, :], e[:, P * j : P * (j + 1)], ident[:])
+
+        def out_unit(x):
+            b, u = divmod(x, 4)
+            if u == 0:
+                result[b] = prep.tile([P, 4, N], F32, name="result_b")
+            dst = result[b][:, :, P * u : P * (u + 1)]
+            src = turned_e[x][:]
+            if x >= 28 and x % 2 == 1:
+                nc.vector.tensor_copy(out=dst, in_=src)
+            else:
+                nc.scalar.copy(out=dst, in_=src)
+            if u % 2 == 1:
+                cols = slice(P * (u - 1), P * (u + 1))
+                nc.sync.dma_start(out=out[b].rearrange("(j p) m -> p j m", p=P)[:, :, cols], in_=result[b][:, :, cols])
+
+        def at(x, work):
+            if 0 <= x < SLOTS:
+                work(x)
+
+        def quantize_at(x, lead, grouped, codes, scales):
+            y = x + lead
+            if 0 <= y < SLOTS and y % 2 == 0:
+                b, u = y // 4, y % 4 // 2
+                quantize(grouped[b], codes[b], scales[b], 256 * u, 256 * (u + 1))
+
+        for g in range(FIRST, SLOTS + 2):
+            at(g + 1, score_matmul)
+            at(g + 7, key_matmuls)
+            at(g - 2, turn_unit)
+            at(g - 2, out_unit)
+            at(g, max_unit)
+            at(g, exp_unit)
+            at(g - 1, recip_unit)
+            at(g + 6, key_unit)
+            if g == FIRST + 2:
+                quantize(w_grouped, w_codes, w_scales, 0, C)
+            quantize_at(g, 10, seg_grouped, seg_codes, seg_scales)
+            at(g - 1, norm_unit)
+            quantize_at(g, 5, q_grouped, q_codes, q_scales)
+            at(g + 11, widen_unit)
+            quantize_at(g, 4, key_grouped, key_codes, key_scales)
+            at(g + 12, seg_unit)
+            at(g + 7, q_unit)

@@ -20,8 +20,8 @@ MAX = mybir.AluOpType.max
 ACT = mybir.ActivationFunctionType
 AX = mybir.AxisListType
 
-SLOTS = 4 * B
-FIRST = -12
+PAIRS = 2 * B
+FIRST = -5
 
 
 def tile_featuremaptransformer_pb_t_kernel(tc, q_ir_bytes, q_ir_scale, irSegF, Wk_dr, bk_dr, out):
@@ -30,10 +30,11 @@ def tile_featuremaptransformer_pb_t_kernel(tc, q_ir_bytes, q_ir_scale, irSegF, W
         keep = ctx.enter_context(tc.tile_pool(name="keep", bufs=1))
         raw = ctx.enter_context(tc.tile_pool(name="raw", bufs=B))
         prep = ctx.enter_context(tc.tile_pool(name="prep", bufs=3))
-        soft = ctx.enter_context(tc.tile_pool(name="soft", bufs=4))
-        ps_s = ctx.enter_context(tc.psum_pool(name="ps_s", bufs=3))
+        gate = ctx.enter_context(tc.tile_pool(name="gate", bufs=1))
+        soft = ctx.enter_context(tc.tile_pool(name="soft", bufs=3))
+        ps_s = ctx.enter_context(tc.psum_pool(name="ps_s", bufs=4))
         ps_k = ctx.enter_context(tc.psum_pool(name="ps_k", bufs=2))
-        ps_t = ctx.enter_context(tc.psum_pool(name="ps_t", bufs=3))
+        ps_t = ctx.enter_context(tc.psum_pool(name="ps_t", bufs=2))
         ctx.enter_context(tc.manual_schedule())
 
         ident = keep.tile([P, P], F32, name="ident")
@@ -41,14 +42,19 @@ def tile_featuremaptransformer_pb_t_kernel(tc, q_ir_bytes, q_ir_scale, irSegF, W
 
         w_raw = keep.tile([P, T, C], BF16, name="w_raw")
         w_rows = Wk_dr.rearrange("(m t) k -> m t k", t=T)
-        for h in range(2):
-            nc.sync.dma_start(out=w_raw[:, 2 * h : 2 * h + 2, :], in_=w_rows[:, 2 * h : 2 * h + 2, :])
         q_scale = keep.tile([P, T], F32, name="q_scale")
         bias = keep.tile([P, T], BF16, name="bias")
         seg_raw, q_raw = [], []
         for b in range(B):
             seg_b = raw.tile([P, T, N], BF16, name="seg_b")
-            nc.sync.dma_start(out=seg_b[:], in_=irSegF[b].rearrange("(p t) h w -> p t (h w)", t=T))
+            seg_rows = irSegF[b].rearrange("(p t) h w -> p t (h w)", t=T)
+            if b == 0:
+                nc.sync.dma_start(out=seg_b[:, :, 0:256], in_=seg_rows[:, :, 0:256])
+                for h in range(2):
+                    nc.sync.dma_start(out=w_raw[:, 2 * h : 2 * h + 2, :], in_=w_rows[:, 2 * h : 2 * h + 2, :])
+                nc.sync.dma_start(out=seg_b[:, :, 256:512], in_=seg_rows[:, :, 256:512])
+            else:
+                nc.sync.dma_start(out=seg_b[:], in_=seg_rows)
             seg_raw.append(seg_b)
             if b == 0:
                 nc.sync.dma_start(out=q_scale[:], in_=q_ir_scale.rearrange("o (p t) x -> p (o t x)", t=T))
@@ -61,169 +67,207 @@ def tile_featuremaptransformer_pb_t_kernel(tc, q_ir_bytes, q_ir_scale, irSegF, W
             nc.vector.quantize_mx(
                 out=codes[:, lo:hi].bitcast(X4),
                 scales=scales[:, lo:hi],
-                in_=grouped[:].rearrange("p c t -> p (c t)")[:, T * lo : T * hi],
+                in_=grouped,
             )
-
-        def interleave(vector, grouped, planes, u):
-            cols = slice(P * u, P * (u + 1))
-            dst = grouped[:, cols, :].rearrange("p (c i) t -> p c t i", i=4)
-            src = planes[:, :, cols].rearrange("p t (c i) -> p c t i", i=4)
-            if vector:
-                nc.vector.tensor_copy(out=dst, in_=src)
-            else:
-                nc.scalar.copy(out=dst, in_=src)
 
         w_grouped = keep.tile([P, C, T], BF16, align_bytes=64, name="w_grouped")
         w_codes = keep.tile([P, C], U32, align_bytes=64, name="w_codes")
         w_scales = keep.tile([P, C], U8, align_bytes=64, name="w_scales")
         w_words = w_grouped[:].rearrange("p o j -> p (o j)").bitcast(F32)
-        for h in range(2):
-            turned = ps_t.tile([P, 4, P], F32, name="turned")
-            for j in range(4):
-                t, u = 2 * h + j // 2, j % 2
-                words = w_raw[:, t, :].bitcast(F32)
-                nc.tensor.transpose(turned[:, j, :], words[:, u : C // 2 : 2], ident[:])
-            dst = w_words[:, 512 * h : 512 * (h + 1)].rearrange("p (t m u) -> p t m u", t=2, u=2)
-            src = turned[:].rearrange("p (t u) m -> p t m u", u=2)
-            if h == 0:
-                nc.scalar.copy(out=dst, in_=src)
-            else:
-                nc.vector.tensor_copy(out=dst, in_=src)
+        def weights():
+            for h in range(2):
+                turned = ps_t.tile([P, 4, P], F32, name="turned")
+                for j in range(4):
+                    t, u = 2 * h + j // 2, j % 2
+                    words = w_raw[:, t, :].bitcast(F32)
+                    nc.tensor.transpose(turned[:, j, :], words[:, u : C // 2 : 2], ident[:])
+                dst = w_words[:, 512 * h : 512 * (h + 1)].rearrange("p (t m u) -> p t m u", t=2, u=2)
+                src = turned[:].rearrange("p (t u) m -> p t m u", u=2)
+                if h == 0:
+                    nc.scalar.copy(out=dst, in_=src)
+                else:
+                    nc.vector.tensor_copy(out=dst, in_=src)
 
         seg_grouped, seg_codes, seg_scales = {}, {}, {}
         q_wide, q_grouped, q_codes, q_scales = {}, {}, {}, {}
         key_psum, key_grouped, key_codes, key_scales = {}, {}, {}, {}
         score, exps, negmax, total, recip, turned_e, result = {}, {}, {}, {}, {}, {}, {}
 
-        def seg_unit(x):
-            b, u = divmod(x, 4)
-            if u == 0:
+        def seg_units(x):
+            b, h = divmod(x, 2)
+            if h == 0:
                 seg_grouped[b] = prep.tile([P, N, T], BF16, align_bytes=64, name="seg_grouped_b")
                 seg_codes[b] = prep.tile([P, N], U32, align_bytes=64, name="seg_codes_b")
                 seg_scales[b] = prep.tile([P, N], U8, align_bytes=64, name="seg_scales_b")
-            interleave(b == 0 and u % 2 == 1, seg_grouped[b], seg_raw[b], u)
+            for i in range(2):
+                u = 2 * h + i
+                cols = slice(P * u, P * (u + 1))
+                dst = seg_grouped[b][:, cols, :].rearrange("p (c i) t -> p c t i", i=4)
+                src = seg_raw[b][:, :, cols].rearrange("p t (c i) -> p c t i", i=4)
+                if b == 0 and i == 1:
+                    nc.vector.tensor_copy(out=dst, in_=src)
+                else:
+                    nc.scalar.copy(out=dst, in_=src)
 
-        def widen_unit(x):
-            b, t = divmod(x, 4)
+        def seg_quantize(x):
+            b, h = divmod(x, 2)
+            lo, hi = 256 * h, 256 * (h + 1)
+            quantize(seg_grouped[b][:, lo:hi, :].rearrange("p c t -> p (c t)"), seg_codes[b], seg_scales[b], lo, hi)
+
+        def widen(x, i):
+            b, h = divmod(x, 2)
+            t = 2 * h + i
             if t == 0:
-                q_wide[b] = prep.tile([P, T, N], BF16, align_bytes=64, name="q_wide_b")
-            nc.vector.tensor_scalar(
-                out=q_wide[b][:, t, :], in0=q_raw[b][:, t, :].bitcast(F8), scalar1=q_scale[:, t : t + 1], scalar2=None, op0=MULT
-            )
+                q_wide[b] = prep.tile([P, T, N], BF16, name="q_wide_b")
+            dst, src, scale = q_wide[b][:, t, :], q_raw[b][:, t, :].bitcast(F8), q_scale[:, t : t + 1]
+            if i == 1 and b > 1:
+                nc.scalar.activation(out=dst, in_=src, func=ACT.Copy, scale=scale)
+            else:
+                nc.vector.tensor_scalar(out=dst, in0=src, scalar1=scale, scalar2=None, op0=MULT)
 
-        def q_unit(x):
-            b, u = divmod(x, 4)
-            if u == 0:
-                q_grouped[b] = prep.tile([P, N, T], BF16, align_bytes=64, name="q_grouped_b")
+        def q_interleave(x):
+            b, h = divmod(x, 2)
+            if h == 0:
                 q_codes[b] = prep.tile([P, N], U32, align_bytes=64, name="q_codes_b")
                 q_scales[b] = prep.tile([P, N], U8, align_bytes=64, name="q_scales_b")
-            interleave(u == 3, q_grouped[b], q_wide[b], u)
+            q_grouped[x] = gate.tile([P, N // 2, T], BF16, align_bytes=64, name="q_grouped_x")
+            src = q_wide[b][:, :, 256 * h : 256 * (h + 1)].rearrange("p t c -> p c t")
+            nc.gpsimd.tensor_scalar(out=q_grouped[x][:], in0=src, scalar1=1.0, scalar2=0.0, op0=MULT, op1=ADD)
+
+        def q_quantize(x):
+            b, h = divmod(x, 2)
+            quantize(q_grouped[x][:].rearrange("p c t -> p (c t)"), q_codes[b], q_scales[b], 256 * h, 256 * (h + 1))
 
         def key_matmuls(x):
-            b, u = divmod(x, 4)
-            key_psum[x] = ps_k.tile([P, T, P], F32, name="key_psum_x")
-            cols = slice(P * u, P * (u + 1))
-            for t in range(T):
+            b, h = divmod(x, 2)
+            for i in range(2):
+                u = 2 * h + i
+                bank = ps_k.tile([P, T, P], F32, name="key_bank")
+                key_psum[(x, i)] = bank
+                cols = slice(P * u, P * (u + 1))
+                for t in range(T):
+                    nc.tensor.matmul_mx(
+                        out=bank[:, t, :],
+                        lhsT=w_codes[:, P * t : P * (t + 1)].bitcast(X4),
+                        lhsT_scale=w_scales[:, P * t : P * (t + 1)],
+                        rhs=seg_codes[b][:, cols].bitcast(X4),
+                        rhs_scale=seg_scales[b][:, cols],
+                        start=True,
+                        stop=True,
+                    )
+
+        def key_units(x):
+            b, h = divmod(x, 2)
+            if h == 0:
+                key_grouped[b] = prep.tile([P, N, T], BF16, align_bytes=64, name="key_grouped_b")
+                key_codes[b] = prep.tile([P, N], U32, align_bytes=64, name="key_codes_b")
+                key_scales[b] = prep.tile([P, N], U8, align_bytes=64, name="key_scales_b")
+            for i in range(2):
+                u = 2 * h + i
+                nc.vector.tensor_tensor(
+                    out=key_grouped[b][:, P * u : P * (u + 1), :],
+                    in0=key_psum[(x, i)][:].rearrange("p t m -> p m t"),
+                    in1=bias[:].unsqueeze(1).to_broadcast([P, P, T]),
+                    op=ADD,
+                )
+
+        def key_quantize(x):
+            b, h = divmod(x, 2)
+            lo, hi = 256 * h, 256 * (h + 1)
+            quantize(key_grouped[b][:, lo:hi, :].rearrange("p c t -> p (c t)"), key_codes[b], key_scales[b], lo, hi)
+
+        def score_matmuls(x):
+            b, h = divmod(x, 2)
+            for i in range(2):
+                u = 2 * h + i
+                bank = ps_s.tile([P, N], F32, name="score_bank")
+                score[(x, i)] = bank
+                cols = slice(P * u, P * (u + 1))
                 nc.tensor.matmul_mx(
-                    out=key_psum[x][:, t, :],
-                    lhsT=w_codes[:, P * t : P * (t + 1)].bitcast(X4),
-                    lhsT_scale=w_scales[:, P * t : P * (t + 1)],
-                    rhs=seg_codes[b][:, cols].bitcast(X4),
-                    rhs_scale=seg_scales[b][:, cols],
+                    out=bank[:],
+                    lhsT=key_codes[b][:, cols].bitcast(X4),
+                    lhsT_scale=key_scales[b][:, cols],
+                    rhs=q_codes[b][:].bitcast(X4),
+                    rhs_scale=q_scales[b][:],
                     start=True,
                     stop=True,
                 )
 
-        def key_unit(x):
-            b, u = divmod(x, 4)
-            if u == 0:
-                key_grouped[b] = prep.tile([P, N, T], BF16, align_bytes=64, name="key_grouped_b")
-                key_codes[b] = prep.tile([P, N], U32, align_bytes=64, name="key_codes_b")
-                key_scales[b] = prep.tile([P, N], U8, align_bytes=64, name="key_scales_b")
-            nc.vector.tensor_tensor(
-                out=key_grouped[b][:, P * u : P * (u + 1), :],
-                in0=key_psum[x][:].rearrange("p t m -> p m t"),
-                in1=bias[:].unsqueeze(1).to_broadcast([P, P, T]),
-                op=ADD,
-            )
+        def max_units(x):
+            negmax[x] = soft.tile([P, 2], F32, name="negmax_x")
+            for i in range(2):
+                nc.vector.tensor_reduce(out=negmax[x][:, i : i + 1], in_=score[(x, i)][:], axis=AX.X, op=MAX, negate=True)
 
-        def score_matmul(x):
-            b, u = divmod(x, 4)
-            score[x] = ps_s.tile([P, N], F32, name="score_x")
-            cols = slice(P * u, P * (u + 1))
-            nc.tensor.matmul_mx(
-                out=score[x][:],
-                lhsT=key_codes[b][:, cols].bitcast(X4),
-                lhsT_scale=key_scales[b][:, cols],
-                rhs=q_codes[b][:].bitcast(X4),
-                rhs_scale=q_scales[b][:],
-                start=True,
-                stop=True,
-            )
-
-        def max_unit(x):
-            negmax[x] = soft.tile([P, 1], F32, name="negmax_x")
-            nc.vector.tensor_reduce(out=negmax[x][:], in_=score[x][:], axis=AX.X, op=MAX, negate=True)
-
-        def exp_unit(x):
-            exps[x] = soft.tile([P, N], F32, name="exps_x")
-            total[x] = soft.tile([P, 1], F32, name="total_x")
-            nc.scalar.activation(
-                out=exps[x][:], in_=score[x][:], func=ACT.Exp, bias=negmax[x][:], scale=1.0, accum_out=total[x][:]
-            )
+        def exp_units(x):
+            exps[x] = soft.tile([P, 2, N], F32, name="exps_x")
+            total[x] = soft.tile([P, 2], F32, name="total_x")
+            for i in range(2):
+                nc.scalar.activation(
+                    out=exps[x][:, i, :],
+                    in_=score[(x, i)][:],
+                    func=ACT.Exp,
+                    bias=negmax[x][:, i : i + 1],
+                    scale=1.0,
+                    accum_out=total[x][:, i : i + 1],
+                )
 
         def recip_unit(x):
-            recip[x] = soft.tile([P, 1], F32, name="recip_x")
+            recip[x] = soft.tile([P, 2], F32, name="recip_x")
             nc.vector.reciprocal(out=recip[x][:], in_=total[x][:])
 
-        def norm_unit(x):
-            nc.vector.tensor_scalar(out=exps[x][:], in0=exps[x][:], scalar1=recip[x][:], scalar2=None, op0=MULT)
+        def norm_units(x):
+            for i in range(2):
+                e = exps[x][:, i, :]
+                if i == 0 and x in (11, 12, 13):
+                    nc.scalar.activation(out=e, in_=e, func=ACT.Copy, scale=recip[x][:, i : i + 1])
+                else:
+                    nc.vector.tensor_scalar(out=e, in0=e, scalar1=recip[x][:, i : i + 1], scalar2=None, op0=MULT)
 
-        def turn_unit(x):
-            turned_e[x] = ps_t.tile([P, 4, P], F32, name="turned")
-            e = exps[x]
-            for j in range(4):
-                nc.tensor.transpose(turned_e[x][:, j, :], e[:, P * j : P * (j + 1)], ident[:])
+        def turn_units(x):
+            for i in range(2):
+                bank = ps_t.tile([P, 4, P], F32, name="turned")
+                turned_e[(x, i)] = bank
+                for j in range(4):
+                    nc.tensor.transpose(bank[:, j, :], exps[x][:, i, P * j : P * (j + 1)], ident[:])
 
-        def out_unit(x):
-            b, u = divmod(x, 4)
-            if u == 0:
+        def out_unit(x, i):
+            b, h = divmod(x, 2)
+            if h == 0 and i == 0:
                 result[b] = prep.tile([P, 4, N], F32, name="result_b")
+            u = 2 * h + i
             dst = result[b][:, :, P * u : P * (u + 1)]
-            src = turned_e[x][:]
-            if x >= 28 and x % 2 == 1:
+            src = turned_e[(x, i)][:]
+            if i == 1 and x >= 14:
                 nc.vector.tensor_copy(out=dst, in_=src)
             else:
                 nc.scalar.copy(out=dst, in_=src)
-            if u % 2 == 1:
-                cols = slice(P * (u - 1), P * (u + 1))
+            if i == 1:
+                cols = slice(256 * h, 256 * (h + 1))
                 nc.sync.dma_start(out=out[b].rearrange("(j p) m -> p j m", p=P)[:, :, cols], in_=result[b][:, :, cols])
 
-        def at(x, work):
-            if 0 <= x < SLOTS:
-                work(x)
+        def at(x, work, *more):
+            if 0 <= x < PAIRS:
+                work(x, *more)
 
-        def quantize_at(x, lead, grouped, codes, scales):
-            y = x + lead
-            if 0 <= y < SLOTS and y % 2 == 0:
-                b, u = y // 4, y % 4 // 2
-                quantize(grouped[b], codes[b], scales[b], 256 * u, 256 * (u + 1))
-
-        for g in range(FIRST, SLOTS + 2):
-            at(g + 1, score_matmul)
-            at(g + 7, key_matmuls)
-            at(g - 2, turn_unit)
-            at(g - 2, out_unit)
-            at(g, max_unit)
-            at(g, exp_unit)
-            at(g - 1, recip_unit)
-            at(g + 6, key_unit)
-            if g == FIRST + 2:
-                quantize(w_grouped, w_codes, w_scales, 0, C)
-            quantize_at(g, 10, seg_grouped, seg_codes, seg_scales)
-            at(g - 1, norm_unit)
-            quantize_at(g, 5, q_grouped, q_codes, q_scales)
-            at(g + 11, widen_unit)
-            quantize_at(g, 4, key_grouped, key_codes, key_scales)
-            at(g + 12, seg_unit)
-            at(g + 7, q_unit)
+        for g in range(FIRST, PAIRS + 1):
+            at(g - 1, turn_units)
+            at(g + 1, score_matmuls)
+            at(g + 3, key_matmuls)
+            at(g + 3, q_interleave)
+            at(g, max_units)
+            at(g, exp_units)
+            at(g - 1, out_unit, 0)
+            at(g - 1, out_unit, 1)
+            at(g + 2, key_units)
+            at(g + 4, seg_quantize)
+            if g == FIRST + 1:
+                quantize(w_grouped[:].rearrange("p c t -> p (c t)"), w_codes, w_scales, 0, C)
+            at(g + 5, seg_units)
+            if g == FIRST:
+                weights()
+            at(g + 5, widen, 0)
+            at(g + 2, key_quantize)
+            at(g, recip_unit)
+            at(g + 5, widen, 1)
+            at(g, norm_units)
+            at(g + 3, q_quantize)

@@ -21,7 +21,7 @@ ACT = mybir.ActivationFunctionType
 AX = mybir.AxisListType
 
 PAIRS = 2 * B
-FIRST = -5
+FIRST = -7
 
 
 def tile_featuremaptransformer_pb_t_kernel(tc, q_ir_bytes, q_ir_scale, irSegF, Wk_dr, bk_dr, out):
@@ -31,7 +31,7 @@ def tile_featuremaptransformer_pb_t_kernel(tc, q_ir_bytes, q_ir_scale, irSegF, W
         raw = ctx.enter_context(tc.tile_pool(name="raw", bufs=B))
         prep = ctx.enter_context(tc.tile_pool(name="prep", bufs=3))
         gate = ctx.enter_context(tc.tile_pool(name="gate", bufs=1))
-        soft = ctx.enter_context(tc.tile_pool(name="soft", bufs=3))
+        soft = ctx.enter_context(tc.tile_pool(name="soft", bufs=4))
         ps_s = ctx.enter_context(tc.psum_pool(name="ps_s", bufs=4))
         ps_k = ctx.enter_context(tc.psum_pool(name="ps_k", bufs=2))
         ps_t = ctx.enter_context(tc.psum_pool(name="ps_t", bufs=2))
@@ -104,15 +104,22 @@ def tile_featuremaptransformer_pb_t_kernel(tc, q_ir_bytes, q_ir_scale, irSegF, W
                 cols = slice(P * u, P * (u + 1))
                 dst = seg_grouped[b][:, cols, :].rearrange("p (c i) t -> p c t i", i=4)
                 src = seg_raw[b][:, :, cols].rearrange("p t (c i) -> p c t i", i=4)
-                if b == 0 and i == 1:
+                if False:
+                    nc.gpsimd.tensor_scalar(
+                        out=seg_grouped[b][:, cols, :],
+                        in0=seg_raw[b][:, :, cols].rearrange("p t c -> p c t"),
+                        scalar1=1.0,
+                        scalar2=0.0,
+                        op0=MULT,
+                        op1=ADD,
+                    )
+                elif b == 0 and i == 1:
                     nc.vector.tensor_copy(out=dst, in_=src)
                 else:
                     nc.scalar.copy(out=dst, in_=src)
 
-        def seg_quantize(x):
-            b, h = divmod(x, 2)
-            lo, hi = 256 * h, 256 * (h + 1)
-            quantize(seg_grouped[b][:, lo:hi, :].rearrange("p c t -> p (c t)"), seg_codes[b], seg_scales[b], lo, hi)
+        def seg_quantize(b):
+            quantize(seg_grouped[b][:].rearrange("p c t -> p (c t)"), seg_codes[b], seg_scales[b], 0, N)
 
         def widen(x, i):
             b, h = divmod(x, 2)
@@ -120,7 +127,7 @@ def tile_featuremaptransformer_pb_t_kernel(tc, q_ir_bytes, q_ir_scale, irSegF, W
             if t == 0:
                 q_wide[b] = prep.tile([P, T, N], BF16, name="q_wide_b")
             dst, src, scale = q_wide[b][:, t, :], q_raw[b][:, t, :].bitcast(F8), q_scale[:, t : t + 1]
-            if i == 1 and b > 1:
+            if b > 1 and (i == 1 or h == 1):
                 nc.scalar.activation(out=dst, in_=src, func=ACT.Copy, scale=scale)
             else:
                 nc.vector.tensor_scalar(out=dst, in0=src, scalar1=scale, scalar2=None, op0=MULT)
@@ -131,8 +138,18 @@ def tile_featuremaptransformer_pb_t_kernel(tc, q_ir_bytes, q_ir_scale, irSegF, W
                 q_codes[b] = prep.tile([P, N], U32, align_bytes=64, name="q_codes_b")
                 q_scales[b] = prep.tile([P, N], U8, align_bytes=64, name="q_scales_b")
             q_grouped[x] = gate.tile([P, N // 2, T], BF16, align_bytes=64, name="q_grouped_x")
-            src = q_wide[b][:, :, 256 * h : 256 * (h + 1)].rearrange("p t c -> p c t")
-            nc.gpsimd.tensor_scalar(out=q_grouped[x][:], in0=src, scalar1=1.0, scalar2=0.0, op0=MULT, op1=ADD)
+            if b > 0:
+                src = q_wide[b][:, :, 256 * h : 256 * (h + 1)].rearrange("p t c -> p c t")
+                nc.gpsimd.tensor_scalar(out=q_grouped[x][:], in0=src, scalar1=1.0, scalar2=0.0, op0=MULT, op1=ADD)
+                return
+            for i in range(2):
+                lo = P * (2 * h + i)
+                src = q_wide[b][:, :, lo : lo + P].rearrange("p t (c i) -> p c t i", i=4)
+                dst = q_grouped[x][:, P * i : P * (i + 1), :].rearrange("p (c i) t -> p c t i", i=4)
+                if i == 1 and h == 1:
+                    nc.vector.tensor_copy(out=dst, in_=src)
+                else:
+                    nc.scalar.copy(out=dst, in_=src)
 
         def q_quantize(x):
             b, h = divmod(x, 2)
@@ -171,10 +188,8 @@ def tile_featuremaptransformer_pb_t_kernel(tc, q_ir_bytes, q_ir_scale, irSegF, W
                     op=ADD,
                 )
 
-        def key_quantize(x):
-            b, h = divmod(x, 2)
-            lo, hi = 256 * h, 256 * (h + 1)
-            quantize(key_grouped[b][:, lo:hi, :].rearrange("p c t -> p (c t)"), key_codes[b], key_scales[b], lo, hi)
+        def key_quantize(b):
+            quantize(key_grouped[b][:].rearrange("p c t -> p (c t)"), key_codes[b], key_scales[b], 0, N)
 
         def score_matmuls(x):
             b, h = divmod(x, 2)
@@ -211,17 +226,17 @@ def tile_featuremaptransformer_pb_t_kernel(tc, q_ir_bytes, q_ir_scale, irSegF, W
                     accum_out=total[x][:, i : i + 1],
                 )
 
-        def recip_unit(x):
-            recip[x] = soft.tile([P, 2], F32, name="recip_x")
-            nc.vector.reciprocal(out=recip[x][:], in_=total[x][:])
+        def recip_unit(x, lo, hi):
+            if lo == 0:
+                recip[x] = soft.tile([P, 2], F32, name="recip_x")
+            nc.vector.reciprocal(out=recip[x][:, lo:hi], in_=total[x][:, lo:hi])
 
-        def norm_units(x):
-            for i in range(2):
-                e = exps[x][:, i, :]
-                if i == 0 and x in (11, 12, 13):
-                    nc.scalar.activation(out=e, in_=e, func=ACT.Copy, scale=recip[x][:, i : i + 1])
-                else:
-                    nc.vector.tensor_scalar(out=e, in0=e, scalar1=recip[x][:, i : i + 1], scalar2=None, op0=MULT)
+        def norm_unit(x, i):
+            e = exps[x][:, i, :]
+            if False:
+                nc.scalar.activation(out=e, in_=e, func=ACT.Copy, scale=recip[x][:, i : i + 1])
+            else:
+                nc.vector.tensor_scalar(out=e, in0=e, scalar1=recip[x][:, i : i + 1], scalar2=None, op0=MULT)
 
         def turn_units(x):
             for i in range(2):
@@ -237,11 +252,14 @@ def tile_featuremaptransformer_pb_t_kernel(tc, q_ir_bytes, q_ir_scale, irSegF, W
             u = 2 * h + i
             dst = result[b][:, :, P * u : P * (u + 1)]
             src = turned_e[(x, i)][:]
-            if i == 1 and x >= 14:
+            if x == 15 and i == 1 or x == 13 and i == 0:
                 nc.vector.tensor_copy(out=dst, in_=src)
             else:
                 nc.scalar.copy(out=dst, in_=src)
-            if i == 1:
+            if x == PAIRS - 1:
+                cols = slice(P * u, P * (u + 1))
+                nc.sync.dma_start(out=out[b].rearrange("(j p) m -> p j m", p=P)[:, :, cols], in_=result[b][:, :, cols])
+            elif i == 1:
                 cols = slice(256 * h, 256 * (h + 1))
                 nc.sync.dma_start(out=out[b].rearrange("(j p) m -> p j m", p=P)[:, :, cols], in_=result[b][:, :, cols])
 
@@ -249,25 +267,28 @@ def tile_featuremaptransformer_pb_t_kernel(tc, q_ir_bytes, q_ir_scale, irSegF, W
             if 0 <= x < PAIRS:
                 work(x, *more)
 
-        for g in range(FIRST, PAIRS + 1):
-            at(g - 1, turn_units)
+        for g in range(FIRST, PAIRS + 2):
             at(g + 1, score_matmuls)
-            at(g + 3, key_matmuls)
+            at(g + 4, key_matmuls)
             at(g + 3, q_interleave)
             at(g, max_units)
+            at(g - 2, out_unit, 0)
             at(g, exp_units)
-            at(g - 1, out_unit, 0)
-            at(g - 1, out_unit, 1)
-            at(g + 2, key_units)
-            at(g + 4, seg_quantize)
+            at(g - 2, out_unit, 1)
+            at(g + 3, key_units)
+            at(g - 1, recip_unit, 0, 2)
+            if g % 2 == 1 and 0 <= g + 5 < PAIRS:
+                seg_quantize((g + 5) // 2)
             if g == FIRST + 1:
                 quantize(w_grouped[:].rearrange("p c t -> p (c t)"), w_codes, w_scales, 0, C)
-            at(g + 5, seg_units)
+            at(g - 1, norm_unit, 0)
+            if g % 2 == 0 and 0 <= g + 2 < PAIRS:
+                key_quantize((g + 2) // 2)
+            at(g + 7, seg_units)
             if g == FIRST:
                 weights()
-            at(g + 5, widen, 0)
-            at(g + 2, key_quantize)
-            at(g, recip_unit)
-            at(g + 5, widen, 1)
-            at(g, norm_units)
+            at(g + 7, widen, 0)
+            at(g - 1, norm_unit, 1)
+            at(g - 1, turn_units)
+            at(g + 7, widen, 1)
             at(g + 3, q_quantize)

@@ -30,7 +30,7 @@ def tile_featuremaptransformer_pb_t_kernel(tc, q_ir_bytes, q_ir_scale, irSegF, W
         keep = ctx.enter_context(tc.tile_pool(name="keep", bufs=1))
         raw = ctx.enter_context(tc.tile_pool(name="raw", bufs=B))
         prep = ctx.enter_context(tc.tile_pool(name="prep", bufs=3))
-        gate = ctx.enter_context(tc.tile_pool(name="gate", bufs=1))
+        gate = ctx.enter_context(tc.tile_pool(name="gate", bufs=2))
         soft = ctx.enter_context(tc.tile_pool(name="soft", bufs=4))
         ps_s = ctx.enter_context(tc.psum_pool(name="ps_s", bufs=4))
         ps_k = ctx.enter_context(tc.psum_pool(name="ps_k", bufs=2))
@@ -99,24 +99,18 @@ def tile_featuremaptransformer_pb_t_kernel(tc, q_ir_bytes, q_ir_scale, irSegF, W
                 seg_grouped[b] = prep.tile([P, N, T], BF16, align_bytes=64, name="seg_grouped_b")
                 seg_codes[b] = prep.tile([P, N], U32, align_bytes=64, name="seg_codes_b")
                 seg_scales[b] = prep.tile([P, N], U8, align_bytes=64, name="seg_scales_b")
-            for i in range(2):
-                u = 2 * h + i
-                cols = slice(P * u, P * (u + 1))
-                dst = seg_grouped[b][:, cols, :].rearrange("p (c i) t -> p c t i", i=4)
-                src = seg_raw[b][:, :, cols].rearrange("p t (c i) -> p c t i", i=4)
-                if False:
-                    nc.gpsimd.tensor_scalar(
-                        out=seg_grouped[b][:, cols, :],
-                        in0=seg_raw[b][:, :, cols].rearrange("p t c -> p c t"),
-                        scalar1=1.0,
-                        scalar2=0.0,
-                        op0=MULT,
-                        op1=ADD,
-                    )
-                elif b == 0 and i == 1:
-                    nc.vector.tensor_copy(out=dst, in_=src)
+            shares = [(nc.scalar, 256 * h, 256)]
+            if b == 0:
+                shares = [(nc.scalar, 256 * h, 128), (nc.vector, 256 * h + 128, 128)]
+            for engine, lo, width in shares:
+                dst = seg_grouped[b][:, lo : lo + width, :].rearrange("p (c i) t -> p c t i", i=4)
+                src = seg_raw[b][:, :, lo : lo + width].rearrange("p t (c i) -> p c t i", i=4)
+                if engine is nc.gpsimd:
+                    engine.tensor_scalar(out=dst, in0=src, scalar1=1.0, scalar2=0.0, op0=MULT, op1=ADD)
+                elif engine is nc.vector:
+                    engine.tensor_copy(out=dst, in_=src)
                 else:
-                    nc.scalar.copy(out=dst, in_=src)
+                    engine.copy(out=dst, in_=src)
 
         def seg_quantize(b):
             quantize(seg_grouped[b][:].rearrange("p c t -> p (c t)"), seg_codes[b], seg_scales[b], 0, N)
@@ -127,7 +121,7 @@ def tile_featuremaptransformer_pb_t_kernel(tc, q_ir_bytes, q_ir_scale, irSegF, W
             if t == 0:
                 q_wide[b] = prep.tile([P, T, N], BF16, name="q_wide_b")
             dst, src, scale = q_wide[b][:, t, :], q_raw[b][:, t, :].bitcast(F8), q_scale[:, t : t + 1]
-            if b > 1 and (i == 1 or h == 1):
+            if b > 1 and (i == 1 or h == 1 and b % 2 == 0):
                 nc.scalar.activation(out=dst, in_=src, func=ACT.Copy, scale=scale)
             else:
                 nc.vector.tensor_scalar(out=dst, in0=src, scalar1=scale, scalar2=None, op0=MULT)
@@ -233,7 +227,7 @@ def tile_featuremaptransformer_pb_t_kernel(tc, q_ir_bytes, q_ir_scale, irSegF, W
 
         def norm_unit(x, i):
             e = exps[x][:, i, :]
-            if False:
+            if i == 1 and x in (9, 10, 11):
                 nc.scalar.activation(out=e, in_=e, func=ACT.Copy, scale=recip[x][:, i : i + 1])
             else:
                 nc.vector.tensor_scalar(out=e, in0=e, scalar1=recip[x][:, i : i + 1], scalar2=None, op0=MULT)
@@ -272,23 +266,23 @@ def tile_featuremaptransformer_pb_t_kernel(tc, q_ir_bytes, q_ir_scale, irSegF, W
             at(g + 4, key_matmuls)
             at(g + 3, q_interleave)
             at(g, max_units)
+            at(g - 1, recip_unit, 0, 2)
             at(g - 2, out_unit, 0)
             at(g, exp_units)
             at(g - 2, out_unit, 1)
             at(g + 3, key_units)
-            at(g - 1, recip_unit, 0, 2)
             if g % 2 == 1 and 0 <= g + 5 < PAIRS:
                 seg_quantize((g + 5) // 2)
-            if g == FIRST + 1:
-                quantize(w_grouped[:].rearrange("p c t -> p (c t)"), w_codes, w_scales, 0, C)
             at(g - 1, norm_unit, 0)
+            at(g - 1, norm_unit, 1)
+            at(g - 1, turn_units)
             if g % 2 == 0 and 0 <= g + 2 < PAIRS:
                 key_quantize((g + 2) // 2)
+            if g == FIRST + 1:
+                quantize(w_grouped[:].rearrange("p c t -> p (c t)"), w_codes, w_scales, 0, C)
             at(g + 7, seg_units)
             if g == FIRST:
                 weights()
             at(g + 7, widen, 0)
-            at(g - 1, norm_unit, 1)
-            at(g - 1, turn_units)
             at(g + 7, widen, 1)
             at(g + 3, q_quantize)

from contextlib import ExitStack

import concourse.mybir as mybir
from concourse.masks import make_identity

B, C, N = 8, 512, 512
FLOPS = 2 * 2 * B * C * C * N

P = 128
T = 4
F32 = mybir.dt.float32
BF16 = mybir.dt.bfloat16
U32 = mybir.dt.uint32
U8 = mybir.dt.uint8
F8 = mybir.dt.float8_e4m3fn
X4 = mybir.dt.float8_e4m3fn_x4
ADD = mybir.AluOpType.add
MULT = mybir.AluOpType.mult
MAX = mybir.AluOpType.max
ACT = mybir.ActivationFunctionType
AX = mybir.AxisListType

PAIRS = 2 * B
FIRST = -7


def tile_featuremaptransformer_pb_t_kernel(tc, q_ir_bytes, q_ir_scale, irSegF, Wk_dr, bk_dr, out):
    nc = tc.nc
    with ExitStack() as ctx:
        keep = ctx.enter_context(tc.tile_pool(name="keep", bufs=1))
        raw = ctx.enter_context(tc.tile_pool(name="raw", bufs=B))
        prep = ctx.enter_context(tc.tile_pool(name="prep", bufs=3))
        gate = ctx.enter_context(tc.tile_pool(name="gate", bufs=2))
        soft = ctx.enter_context(tc.tile_pool(name="soft", bufs=4))
        ps_s = ctx.enter_context(tc.psum_pool(name="ps_s", bufs=4))
        ps_k = ctx.enter_context(tc.psum_pool(name="ps_k", bufs=2))
        ps_t = ctx.enter_context(tc.psum_pool(name="ps_t", bufs=2))
        ctx.enter_context(tc.manual_schedule())

        ident = keep.tile([P, P], F32, name="ident")
        make_identity(nc, ident[:])

        w_raw = keep.tile([P, T, C], BF16, name="w_raw")
        w_rows = Wk_dr.rearrange("(m t) k -> m t k", t=T)
        q_scale = keep.tile([P, T], F32, name="q_scale")
        bias = keep.tile([P, T], BF16, name="bias")
        seg_raw, q_raw = [], []
        for b in range(B):
            seg_b = raw.tile([P, T, N], BF16, name="seg_b")
            seg_rows = irSegF[b].rearrange("(p t) h w -> p t (h w)", t=T)
            if b == 0:
                nc.sync.dma_start(out=seg_b[:, :, 0:256], in_=seg_rows[:, :, 0:256])
                for h in range(2):
                    nc.sync.dma_start(out=w_raw[:, 2 * h : 2 * h + 2, :], in_=w_rows[:, 2 * h : 2 * h + 2, :])
                nc.sync.dma_start(out=seg_b[:, :, 256:512], in_=seg_rows[:, :, 256:512])
            else:
                nc.sync.dma_start(out=seg_b[:], in_=seg_rows)
            seg_raw.append(seg_b)
            if b == 0:
                nc.sync.dma_start(out=q_scale[:], in_=q_ir_scale.rearrange("o (p t) x -> p (o t x)", t=T))
                nc.sync.dma_start(out=bias[:], in_=bk_dr.rearrange("(p t) -> p t", t=T))
            q_b = raw.tile([P, T, N], U8, name="q_b")
            nc.sync.dma_start(out=q_b[:], in_=q_ir_bytes[b].rearrange("(p t) n -> p t n", t=T))
            q_raw.append(q_b)

        def quantize(grouped, codes, scales, lo, hi):
            nc.vector.quantize_mx(
                out=codes[:, lo:hi].bitcast(X4),
                scales=scales[:, lo:hi],
                in_=grouped,
            )

        w_grouped = keep.tile([P, C, T], BF16, align_bytes=64, name="w_grouped")
        w_codes = keep.tile([P, C], U32, align_bytes=64, name="w_codes")
        w_scales = keep.tile([P, C], U8, align_bytes=64, name="w_scales")
        w_words = w_grouped[:].rearrange("p o j -> p (o j)").bitcast(F32)
        def weights():
            for h in range(2):
                turned = ps_t.tile([P, 4, P], F32, name="turned")
                for j in range(4):
                    t, u = 2 * h + j // 2, j % 2
                    words = w_raw[:, t, :].bitcast(F32)
                    nc.tensor.transpose(turned[:, j, :], words[:, u : C // 2 : 2], ident[:])
                dst = w_words[:, 512 * h : 512 * (h + 1)].rearrange("p (t m u) -> p t m u", t=2, u=2)
                src = turned[:].rearrange("p (t u) m -> p t m u", u=2)
                if h == 0:
                    nc.scalar.copy(out=dst, in_=src)
                else:
                    nc.vector.tensor_copy(out=dst, in_=src)

        seg_grouped, seg_codes, seg_scales = {}, {}, {}
        q_wide, q_grouped, q_codes, q_scales = {}, {}, {}, {}
        key_psum, key_grouped, key_codes, key_scales = {}, {}, {}, {}
        score, exps, negmax, total, recip, turned_e, result = {}, {}, {}, {}, {}, {}, {}

        def seg_units(x):
            b, h = divmod(x, 2)
            if h == 0:
                seg_grouped[b] = prep.tile([P, N, T], BF16, align_bytes=64, name="seg_grouped_b")
                seg_codes[b] = prep.tile([P, N], U32, align_bytes=64, name="seg_codes_b")
                seg_scales[b] = prep.tile([P, N], U8, align_bytes=64, name="seg_scales_b")
            shares = [(nc.scalar, 256 * h, 256)]
            if b == 0:
                shares = [(nc.scalar, 256 * h, 128), (nc.vector, 256 * h + 128, 128)]
            for engine, lo, width in shares:
                dst = seg_grouped[b][:, lo : lo + width, :].rearrange("p (c i) t -> p c t i", i=4)
                src = seg_raw[b][:, :, lo : lo + width].rearrange("p t (c i) -> p c t i", i=4)
                if engine is nc.gpsimd:
                    engine.tensor_scalar(out=dst, in0=src, scalar1=1.0, scalar2=0.0, op0=MULT, op1=ADD)
                elif engine is nc.vector:
                    engine.tensor_copy(out=dst, in_=src)
                else:
                    engine.copy(out=dst, in_=src)

        def seg_quantize(b):
            quantize(seg_grouped[b][:].rearrange("p c t -> p (c t)"), seg_codes[b], seg_scales[b], 0, N)

        def widen(x, i):
            b, h = divmod(x, 2)
            t = 2 * h + i
            if t == 0:
                q_wide[b] = prep.tile([P, T, N], BF16, name="q_wide_b")
            dst, src, scale = q_wide[b][:, t, :], q_raw[b][:, t, :].bitcast(F8), q_scale[:, t : t + 1]
            if b > 1 and (i == 1 or h == 1 and b % 2 == 0):
                nc.scalar.activation(out=dst, in_=src, func=ACT.Copy, scale=scale)
            else:
                nc.vector.tensor_scalar(out=dst, in0=src, scalar1=scale, scalar2=None, op0=MULT)

        def q_interleave(x):
            b, h = divmod(x, 2)
            if h == 0:
                q_codes[b] = prep.tile([P, N], U32, align_bytes=64, name="q_codes_b")
                q_scales[b] = prep.tile([P, N], U8, align_bytes=64, name="q_scales_b")
            q_grouped[x] = gate.tile([P, N // 2, T], BF16, align_bytes=64, name="q_grouped_x")
            if b > 0:
                src = q_wide[b][:, :, 256 * h : 256 * (h + 1)].rearrange("p t c -> p c t")
                nc.gpsimd.tensor_scalar(out=q_grouped[x][:], in0=src, scalar1=1.0, scalar2=0.0, op0=MULT, op1=ADD)
                return
            for i in range(2):
                lo = P * (2 * h + i)
                src = q_wide[b][:, :, lo : lo + P].rearrange("p t (c i) -> p c t i", i=4)
                dst = q_grouped[x][:, P * i : P * (i + 1), :].rearrange("p (c i) t -> p c t i", i=4)
                if i == 1 and h == 1:
                    nc.vector.tensor_copy(out=dst, in_=src)
                else:
                    nc.scalar.copy(out=dst, in_=src)

        def q_quantize(x):
            b, h = divmod(x, 2)
            quantize(q_grouped[x][:].rearrange("p c t -> p (c t)"), q_codes[b], q_scales[b], 256 * h, 256 * (h + 1))

        def key_matmuls(x):
            b, h = divmod(x, 2)
            for i in range(2):
                u = 2 * h + i
                bank = ps_k.tile([P, T, P], F32, name="key_bank")
                key_psum[(x, i)] = bank
                cols = slice(P * u, P * (u + 1))
                for t in range(T):
                    nc.tensor.matmul_mx(
                        out=bank[:, t, :],
                        lhsT=w_codes[:, P * t : P * (t + 1)].bitcast(X4),
                        lhsT_scale=w_scales[:, P * t : P * (t + 1)],
                        rhs=seg_codes[b][:, cols].bitcast(X4),
                        rhs_scale=seg_scales[b][:, cols],
                        start=True,
                        stop=True,
                    )

        def key_units(x):
            b, h = divmod(x, 2)
            if h == 0:
                key_grouped[b] = prep.tile([P, N, T], BF16, align_bytes=64, name="key_grouped_b")
                key_codes[b] = prep.tile([P, N], U32, align_bytes=64, name="key_codes_b")
                key_scales[b] = prep.tile([P, N], U8, align_bytes=64, name="key_scales_b")
            for i in range(2):
                u = 2 * h + i
                nc.vector.tensor_tensor(
                    out=key_grouped[b][:, P * u : P * (u + 1), :],
                    in0=key_psum[(x, i)][:].rearrange("p t m -> p m t"),
                    in1=bias[:].unsqueeze(1).to_broadcast([P, P, T]),
                    op=ADD,
                )

        def key_quantize(b):
            quantize(key_grouped[b][:].rearrange("p c t -> p (c t)"), key_codes[b], key_scales[b], 0, N)

        def score_matmuls(x):
            b, h = divmod(x, 2)
            for i in range(2):
                u = 2 * h + i
                bank = ps_s.tile([P, N], F32, name="score_bank")
                score[(x, i)] = bank
                cols = slice(P * u, P * (u + 1))
                nc.tensor.matmul_mx(
                    out=bank[:],
                    lhsT=key_codes[b][:, cols].bitcast(X4),
                    lhsT_scale=key_scales[b][:, cols],
                    rhs=q_codes[b][:].bitcast(X4),
                    rhs_scale=q_scales[b][:],
                    start=True,
                    stop=True,
                )

        def max_units(x):
            negmax[x] = soft.tile([P, 2], F32, name="negmax_x")
            for i in range(2):
                nc.vector.tensor_reduce(out=negmax[x][:, i : i + 1], in_=score[(x, i)][:], axis=AX.X, op=MAX, negate=True)

        def exp_units(x):
            exps[x] = soft.tile([P, 2, N], F32, name="exps_x")
            total[x] = soft.tile([P, 2], F32, name="total_x")
            for i in range(2):
                nc.scalar.activation(
                    out=exps[x][:, i, :],
                    in_=score[(x, i)][:],
                    func=ACT.Exp,
                    bias=negmax[x][:, i : i + 1],
                    scale=1.0,
                    accum_out=total[x][:, i : i + 1],
                )

        def recip_unit(x, lo, hi):
            if lo == 0:
                recip[x] = soft.tile([P, 2], F32, name="recip_x")
            nc.vector.reciprocal(out=recip[x][:, lo:hi], in_=total[x][:, lo:hi])

        def norm_unit(x, i):
            e = exps[x][:, i, :]
            if i == 1 and x in (9, 10, 11):
                nc.scalar.activation(out=e, in_=e, func=ACT.Copy, scale=recip[x][:, i : i + 1])
            else:
                nc.vector.tensor_scalar(out=e, in0=e, scalar1=recip[x][:, i : i + 1], scalar2=None, op0=MULT)

        def turn_units(x):
            for i in range(2):
                bank = ps_t.tile([P, 4, P], F32, name="turned")
                turned_e[(x, i)] = bank
                for j in range(4):
                    nc.tensor.transpose(bank[:, j, :], exps[x][:, i, P * j : P * (j + 1)], ident[:])

        def out_unit(x, i):
            b, h = divmod(x, 2)
            if h == 0 and i == 0:
                result[b] = prep.tile([P, 4, N], F32, name="result_b")
            u = 2 * h + i
            dst = result[b][:, :, P * u : P * (u + 1)]
            src = turned_e[(x, i)][:]
            if x == 15 and i == 1 or x == 13 and i == 0:
                nc.vector.tensor_copy(out=dst, in_=src)
            else:
                nc.scalar.copy(out=dst, in_=src)
            if x == PAIRS - 1:
                cols = slice(P * u, P * (u + 1))
                nc.sync.dma_start(out=out[b].rearrange("(j p) m -> p j m", p=P)[:, :, cols], in_=result[b][:, :, cols])
            elif i == 1:
                cols = slice(256 * h, 256 * (h + 1))
                nc.sync.dma_start(out=out[b].rearrange("(j p) m -> p j m", p=P)[:, :, cols], in_=result[b][:, :, cols])

        def at(x, work, *more):
            if 0 <= x < PAIRS:
                work(x, *more)

        for g in range(FIRST, PAIRS + 2):
            at(g + 1, score_matmuls)
            at(g + 4, key_matmuls)
            at(g + 3, q_interleave)
            at(g, max_units)
            at(g - 1, recip_unit, 0, 2)
            at(g - 2, out_unit, 0)
            at(g, exp_units)
            at(g - 2, out_unit, 1)
            at(g + 3, key_units)
            if g % 2 == 1 and 0 <= g + 5 < PAIRS:
                seg_quantize((g + 5) // 2)
            at(g - 1, norm_unit, 0)
            at(g - 1, norm_unit, 1)
            at(g - 1, turn_units)
            if g % 2 == 0 and 0 <= g + 2 < PAIRS:
                key_quantize((g + 2) // 2)
            if g == FIRST + 1:
                quantize(w_grouped[:].rearrange("p c t -> p (c t)"), w_codes, w_scales, 0, C)
            at(g + 7, seg_units)
            if g == FIRST:
                weights()
            at(g + 7, widen, 0)
            at(g + 7, widen, 1)
            at(g + 3, q_quantize)
